import numpy as np
import ml_dtypes


def mxq(x, axis, fmt="e4m3"):
    dtype, down = {"e4m3": (ml_dtypes.float8_e4m3fn, 7), "e5m2": (ml_dtypes.float8_e5m2, 14)}[fmt]
    v = np.moveaxis(np.asarray(x, np.float32).astype(ml_dtypes.bfloat16).astype(np.float64), axis, -1)
    blocks = v.reshape(v.shape[:-1] + (-1, 32))
    amax = np.abs(blocks).max(-1, keepdims=True)
    byte = np.maximum(np.where(amax > 0, np.frexp(amax)[1] - 1 + 127, 0) - down, 1)
    scale = np.exp2(byte - 127.0)
    codes = (blocks / scale).astype(np.float32).astype(dtype).astype(np.float64)
    return np.moveaxis((codes * scale).reshape(v.shape), -1, axis)


WIDE = False


def mx_kscale(k):
    if not WIDE:
        return np.ones(k)
    levels = np.array([10, -10, 5, -5, 0])
    a = np.random.permutation(np.resize(levels, k // 512 * 4)).reshape(k // 512, 4)
    idx = np.arange(k)
    return np.exp2(a[idx // 512, idx % 128 // 32])


BF16 = ml_dtypes.bfloat16


def bf(x):
    return np.asarray(x, np.float32).astype(BF16)


def f64(x):
    return np.asarray(x).astype(np.float64)


E2M1 = np.array([0.0, 0.5, 1.0, 1.5, 2.0, 3.0, 4.0, 6.0, -0.0, -0.5, -1.0, -1.5, -2.0, -3.0, -4.0, -6.0])


def pack_weight(w, fmt):
    k, n = w.shape
    w = f64(bf(w)).reshape(k // 32, 32, n)
    amax = np.abs(w).max(1)
    if fmt == "e4m3":
        byte = np.frexp(amax)[1] - 1 + 127 - 7
    else:
        mant, ex = np.frexp(amax / 6.0)
        byte = np.where(mant > 0.5, ex, ex - 1) + 127
    byte = np.clip(np.where(amax > 0, byte, 1), 1, 254)
    scaled = (w * np.exp2(127.0 - byte)[:, None, :]).reshape(k, n).astype(np.float32)
    by_word = np.ascontiguousarray(scaled.reshape(k // 512, 128, 4, n).transpose(0, 1, 3, 2))
    if fmt == "e4m3":
        words = by_word.astype(ml_dtypes.float8_e4m3fn).view(np.uint8)
    else:
        c = by_word.astype(ml_dtypes.float4_e2m1fn).view(np.uint8) & 0xF
        words = c[..., 0::2] | (c[..., 1::2] << 4)
    return np.ascontiguousarray(words), np.ascontiguousarray(byte.astype(np.uint8).reshape(k // 512, 16, n))


def unpack_weight(words, scales, fmt):
    g, p, n, _ = words.shape
    if fmt == "e4m3":
        vals = np.ascontiguousarray(words).view(ml_dtypes.float8_e4m3fn).astype(np.float64)
    else:
        nib = np.empty((g, p, n, 4), np.uint8)
        nib[..., 0::2] = words & 0xF
        nib[..., 1::2] = words >> 4
        vals = E2M1[nib]
    vals = vals * np.repeat(np.exp2(scales.astype(np.float64) - 127.0), 8, axis=1)[..., None]
    return vals.transpose(0, 1, 3, 2).reshape(g * 512, n)


B, D, T, DEPTH, LD = 512, 1024, 128, 6, 128
NI = 2 ** DEPTH - 1
NL = 2 ** DEPTH


def sigmoid(v):
    return 1.0 / (1.0 + np.exp(-v))


def setup_inputs():
    s = mx_kscale(D)
    x = bf(np.random.standard_normal((B, D)) * s)
    stack = np.random.standard_normal((NI, T, D)) / np.sqrt(D) / s
    cat = np.ascontiguousarray(stack.swapaxes(1, 2)).reshape(-1, T)
    words, scales = pack_weight(cat, "e4m3")
    return {"x": x,
            "W_words": words,
            "W_scales": scales,
            "b": bf(np.random.standard_normal((NI, T)) * 0.5),
            "leaf_w": bf(np.random.standard_normal((NL, LD, T)) / np.sqrt(T * 0.6 ** DEPTH))}


def reference(x, W_words, W_scales, b, leaf_w):
    wst = unpack_weight(W_words, W_scales, "e4m3").reshape(NI, D, T)
    z = (mxq(f64(x), 1, "e4m3") @ wst.transpose(1, 0, 2).reshape(D, NI * T)).reshape(B, NI, T) + f64(b)
    gates = sigmoid(z)
    probs = np.ones((B, 1, T))
    for l in range(DEPTH):
        g = gates[:, 2 ** l - 1: 2 ** (l + 1) - 1]
        probs = np.stack([probs * g, probs * (1.0 - g)], axis=2).reshape(B, 2 ** (l + 1), T)
    lw = f64(leaf_w).transpose(0, 2, 1).reshape(NL * T, LD)
    return mxq(probs.reshape(B, NL * T), 1, "e4m3") @ mxq(lw, 0, "e4m3")

@@ -1,0 +1,263 @@
+from contextlib import ExitStack
+
+import concourse.mybir as mybir
+from concourse.masks import make_identity
+
+F32 = mybir.dt.float32
+BF16 = mybir.dt.bfloat16
+I32 = mybir.dt.int32
+U32 = mybir.dt.uint32
+U8 = mybir.dt.uint8
+FP8X4 = mybir.dt.float8_e4m3fn_x4
+SIGMOID = mybir.ActivationFunctionType.Sigmoid
+MULT = mybir.AluOpType.mult
+
+P = 128
+PACK = 4
+K_PASS = P * PACK
+
+BATCH, FEATURES, TREES, DEPTH, OUT_COLS = 512, 1024, 128, 6, 128
+NODES = 2**DEPTH - 1
+LEAVES = 2**DEPTH
+HALVES = FEATURES // K_PASS
+BATCH_TILES = BATCH // P
+
+BLOCK_DEPTH = 3
+BLOCK_NODES = 2**BLOCK_DEPTH - 1
+BLOCK_OUTPUTS = 2**BLOCK_DEPTH
+BLOCKS = 1 + BLOCK_OUTPUTS
+BLOCK_PASSES = BLOCK_OUTPUTS // PACK
+LEAF_PASSES = LEAVES // PACK
+LOADS_AHEAD = 3
+
+FLOPS = 2 * BATCH * FEATURES * NODES * TREES + 2 * BATCH * LEAVES * TREES * OUT_COLS
+
+
+def first_node(block, level):
+    if block == 0:
+        return 2**level - 1
+    return 2 ** (BLOCK_DEPTH + level) - 1 + (block - 1) * 2**level
+
+
+def tile_softtreeensemble_pa_e_kernel(tc, x, W_words, W_scales, b, leaf_w, out):
+    nc = tc.nc
+    with ExitStack() as ctx:
+        const = ctx.enter_context(tc.tile_pool(name="const", bufs=1))
+        x_pool = ctx.enter_context(tc.tile_pool(name="x_pool", bufs=BATCH_TILES))
+        w_pool = ctx.enter_context(tc.tile_pool(name="w_pool", bufs=LOADS_AHEAD + 1))
+        lw_pool = ctx.enter_context(tc.tile_pool(name="lw_pool", bufs=2))
+        gate_pool = ctx.enter_context(tc.tile_pool(name="gate_pool", bufs=2))
+        prob_pool = ctx.enter_context(tc.tile_pool(name="prob_pool", bufs=2))
+        leaf_pool = ctx.enter_context(tc.tile_pool(name="leaf_pool", bufs=2 * BLOCK_PASSES))
+        acc_pool = ctx.enter_context(tc.psum_pool(name="acc_pool", bufs=1))
+        bank_pool = ctx.enter_context(tc.psum_pool(name="bank_pool", bufs=4))
+
+        ident_f32 = const.tile([P, P], F32)
+        make_identity(nc, ident_f32[:])
+        ident_bf16 = const.tile([P, P], BF16)
+        make_identity(nc, ident_bf16[:])
+        warm = const.tile([P, 1], F32)
+        nc.vector.memset(warm[:], 0.0)
+        nc.scalar.activation(out=warm[:], in_=warm[:], func=SIGMOID)
+
+        x_rows = []
+        for bt in range(BATCH_TILES):
+            x_sb = x_pool.tile([P, FEATURES], BF16, name="x_sb")
+            nc.sync.dma_start(out=x_sb[:], in_=x[bt * P : (bt + 1) * P, :])
+            x_rows.append(x_sb)
+
+        b_rows = const.tile([P, P], BF16)
+        nc.vector.memset(b_rows[:], 0.0)
+        nc.scalar.dma_start(out=b_rows[:NODES, :], in_=b)
+
+        w_planes = const.tile([P, HALVES * NODES, TREES], U8, align_bytes=64)
+
+        def load_scale_rows(node, count):
+            groups = slice(HALVES * node, HALVES * (node + count))
+            nc.vector.memset(w_planes[:, groups, :].bitcast(I32), 0)
+            for quad in range(4):
+                nc.sync.dma_start(
+                    out=w_planes[32 * quad : 32 * quad + 4, groups, :].bitcast(I32),
+                    in_=W_scales[groups, 4 * quad : 4 * quad + 4, :].rearrange("g r n -> r g n").bitcast(I32),
+                )
+
+        def load_block(block):
+            w_words = w_pool.tile([P, BLOCK_NODES, HALVES, TREES], U32, name="w_words", align_bytes=64)
+            for level in range(BLOCK_DEPTH):
+                count = 2**level
+                node = first_node(block, level)
+                if block == 1:
+                    load_scale_rows(node, count * BLOCK_OUTPUTS)
+                nc.sync.dma_start(
+                    out=w_words[:, count - 1 : 2 * count - 1, :, :].rearrange("p m h n -> p (m h) n").bitcast(I32),
+                    in_=W_words[HALVES * node : HALVES * (node + count)]
+                    .rearrange("g p n t -> p g (n t)")
+                    .bitcast(I32),
+                )
+            if block == 0:
+                return w_words, None
+            lw_sb = w_pool.tile([P, BLOCK_OUTPUTS, TREES], BF16, name="lw_sb")
+            first_leaf = (block - 1) * BLOCK_OUTPUTS
+            nc.sync.dma_start(
+                out=lw_sb[:], in_=leaf_w[first_leaf : first_leaf + BLOCK_OUTPUTS].rearrange("j c t -> c j t")
+            )
+            return w_words, lw_sb
+
+        load_scale_rows(0, BLOCK_NODES)
+        loaded = [load_block(block) for block in range(LOADS_AHEAD)]
+
+        x_codes = const.tile([P, HALVES, BATCH], U32, align_bytes=64)
+        x_scales = const.tile([P, HALVES, BATCH], U8, align_bytes=64)
+        for bt in range(BATCH_TILES):
+            x_words = x_rows[bt][:].bitcast(F32)
+            xT = bank_pool.tile([P, HALVES, 2, P], F32, tag="bank")
+            for h in range(HALVES):
+                for u in range(2):
+                    nc.tensor.transpose(
+                        xT[:, h, u, :], x_words[:, 256 * h + u : 256 * (h + 1) : 2], ident_f32[:]
+                    )
+            x_grouped = x_pool.tile([P, HALVES, P * PACK], BF16, name="x_grouped", align_bytes=64)
+            grouped_words = x_grouped[:].bitcast(F32).rearrange("p h (i u) -> p h i u", u=2)
+            if bt % 2 == 0:
+                nc.vector.tensor_copy(out=grouped_words, in_=xT[:].rearrange("p h u i -> p h i u"))
+            else:
+                nc.scalar.copy(out=grouped_words, in_=xT[:].rearrange("p h u i -> p h i u"))
+            cols = slice(bt * P, (bt + 1) * P)
+            for h in range(HALVES):
+                nc.vector.quantize_mx(
+                    out=x_codes[:, h, cols].bitcast(FP8X4), scales=x_scales[:, h, cols], in_=x_grouped[:, h, :]
+                )
+
+        bT = bank_pool.tile([P, P], BF16, tag="bank")
+        nc.tensor.transpose(bT[:], b_rows[:], ident_bf16[:])
+        bias = const.tile([P, P], F32)
+        nc.vector.tensor_copy(out=bias[:], in_=bT[:])
+        bias_negated = const.tile([P, P], F32)
+        nc.vector.tensor_scalar_mul(out=bias_negated[:], in0=bT[:], scalar1=-1.0)
+
+        def gate_block(block, w_words):
+            gates = []
+            for level in range(BLOCK_DEPTH):
+                count = 2**level
+                both = (block == 0 and level == 0) or (block > 0 and level == BLOCK_DEPTH - 1)
+                gate = gate_pool.tile([P, count, 2 if both else 1, BATCH], F32, name="gate%d" % level)
+                for j in range(count):
+                    node = first_node(block, level) + j
+                    z = bank_pool.tile([P, BATCH], F32, tag="bank")
+                    for h in range(HALVES):
+                        nc.tensor.matmul_mx(
+                            out=z[:],
+                            lhsT=w_words[:, count - 1 + j, h, :].bitcast(FP8X4),
+                            lhsT_scale=w_planes[:, HALVES * node + h, :],
+                            rhs=x_codes[:, h, :].bitcast(FP8X4),
+                            rhs_scale=x_scales[:, h, :],
+                            start=(h == 0),
+                            stop=(h == HALVES - 1),
+                        )
+                    nc.scalar.activation(
+                        out=gate[:, j, 0, :], in_=z[:], func=SIGMOID, bias=bias[:, node : node + 1], scale=1.0
+                    )
+                    if both:
+                        nc.scalar.activation(
+                            out=gate[:, j, 1, :],
+                            in_=z[:],
+                            func=SIGMOID,
+                            bias=bias_negated[:, node : node + 1],
+                            scale=-1.0,
+                        )
+                gates.append(gate)
+            return gates
+
+        def quantise_leaf_weights(lw_sb):
+            lwT = bank_pool.tile([P, BLOCK_OUTPUTS, OUT_COLS], BF16, tag="bank")
+            for j in range(BLOCK_OUTPUTS):
+                nc.tensor.transpose(lwT[:, j, :], lw_sb[:, j, :], ident_bf16[:])
+            lw_grouped = lw_pool.tile([P, BLOCK_PASSES, OUT_COLS * PACK], BF16, name="lw_grouped", align_bytes=64)
+            nc.scalar.copy(
+                out=lw_grouped[:].rearrange("p q (c t) -> p q c t", t=PACK),
+                in_=lwT[:].rearrange("p (q t) c -> p q c t", t=PACK),
+            )
+            lw_codes = lw_pool.tile([P, BLOCK_PASSES * OUT_COLS], U32, name="lw_codes", align_bytes=64)
+            lw_scales = lw_pool.tile([P, BLOCK_PASSES * OUT_COLS], U8, name="lw_scales", align_bytes=64)
+            nc.vector.quantize_mx(
+                out=lw_codes[:].bitcast(FP8X4), scales=lw_scales[:], in_=lw_grouped[:].rearrange("p q n -> p (q n)")
+            )
+            return lw_codes, lw_scales
+
+        def split(parents, gate, kids):
+            nc.vector.tensor_mul(out=kids[:, :, 0, :], in0=parents, in1=gate[:, :, 0, :])
+            nc.vector.tensor_sub(out=kids[:, :, 1, :], in0=parents, in1=kids[:, :, 0, :])
+
+        def as_row(kids):
+            return kids[:].rearrange("p j s i -> p (j s) i")
+
+        level3 = const.tile([P, BLOCK_OUTPUTS // 2, 2, BATCH], F32)
+
+        def top_block(gates):
+            kids1 = prob_pool.tile([P, 2, 2, BATCH], F32, name="kids1")
+            split(as_row(gates[0]), gates[1], kids1)
+            split(as_row(kids1), gates[2], level3)
+
+        def leaf_block(block, gates):
+            kids0 = prob_pool.tile([P, 1, 2, BATCH], F32, name="kids0")
+            split(as_row(level3)[:, block - 1 : block, :], gates[0], kids0)
+            kids1 = prob_pool.tile([P, 2, 2, BATCH], F32, name="kids1")
+            split(as_row(kids0), gates[1], kids1)
+            quantised = []
+            for q in range(BLOCK_PASSES):
+                pair = slice(2 * q, 2 * q + 2)
+                p6_grouped = leaf_pool.tile([P, BATCH * PACK], BF16, name="p6_grouped", align_bytes=64)
+                nc.vector.tensor_tensor(
+                    out=p6_grouped[:].rearrange("p (i a s) -> p i a s", a=2, s=2),
+                    in0=as_row(kids1)[:, pair, :].rearrange("p a i -> p i a").unsqueeze(3).to_broadcast([P, BATCH, 2, 2]),
+                    in1=gates[2][:, pair, :, :].rearrange("p a s i -> p i a s"),
+                    op=MULT,
+                )
+                quantised.append(p6_grouped)
+            words = []
+            for q in range(BLOCK_PASSES):
+                p6_codes = leaf_pool.tile([P, BATCH], U32, name="p6_codes", align_bytes=64)
+                p6_scales = leaf_pool.tile([P, BATCH], U8, name="p6_scales", align_bytes=64)
+                nc.vector.quantize_mx(out=p6_codes[:].bitcast(FP8X4), scales=p6_scales[:], in_=quantised[q][:])
+                words.append((p6_codes, p6_scales))
+            return words
+
+        acc = [acc_pool.tile([P, BATCH], F32, name="acc%d" % bt) for bt in range(BATCH_TILES)]
+
+        def second_matmul(block, words, lw_codes, lw_scales):
+            for q in range(BLOCK_PASSES):
+                leaf_pass = (block - 1) * BLOCK_PASSES + q
+                p6_codes, p6_scales = words[q]
+                out_cols = slice(q * OUT_COLS, (q + 1) * OUT_COLS)
+                for bt in range(BATCH_TILES):
+                    rows = slice(bt * P, (bt + 1) * P)
+                    nc.tensor.matmul_mx(
+                        out=acc[bt][:, :OUT_COLS],
+                        lhsT=p6_codes[:, rows].bitcast(FP8X4),
+                        lhsT_scale=p6_scales[:, rows],
+                        rhs=lw_codes[:, out_cols].bitcast(FP8X4),
+                        rhs_scale=lw_scales[:, out_cols],
+                        start=(leaf_pass == 0),
+                        stop=(leaf_pass == LEAF_PASSES - 1),
+                    )
+
+        gates = gate_block(0, loaded[0][0])
+        for block in range(BLOCKS):
+            if block + LOADS_AHEAD < BLOCKS:
+                loaded.append(load_block(block + LOADS_AHEAD))
+            if block + 1 < BLOCKS:
+                next_gates = gate_block(block + 1, loaded[block + 1][0])
+                next_lw = quantise_leaf_weights(loaded[block + 1][1])
+            if block == 0:
+                top_block(gates)
+            else:
+                second_matmul(block, leaf_block(block, gates), lw[0], lw[1])
+            gates, lw = next_gates, next_lw
+
+        out_sb = const.tile([P, BATCH_TILES, OUT_COLS], F32)
+        for bt in range(BATCH_TILES):
+            if bt % 2 == 0:
+                nc.vector.tensor_copy(out=out_sb[:, bt, :], in_=acc[bt][:, :OUT_COLS])
+            else:
+                nc.scalar.copy(out=out_sb[:, bt, :], in_=acc[bt][:, :OUT_COLS])
+        nc.sync.dma_start(out=out.rearrange("(bt p) c -> p bt c", p=P), in_=out_sb[:])

@@ -27,6 +27,7 @@ BLOCK_NODES = 2**BLOCK_DEPTH - 1
 BLOCK_OUTPUTS = 2**BLOCK_DEPTH
 BLOCKS = 1 + BLOCK_OUTPUTS
 BLOCK_PASSES = BLOCK_OUTPUTS // PACK
+RUN = 4
 LEAF_PASSES = LEAVES // PACK
 LOADS_AHEAD = 3
 
@@ -175,7 +176,7 @@ def tile_softtreeensemble_pa_e_kernel(tc, x, W_words, W_scales, b, leaf_w, out):
             lw_grouped = lw_pool.tile([P, BLOCK_PASSES, OUT_COLS * PACK], BF16, name="lw_grouped", align_bytes=64)
             nc.scalar.copy(
                 out=lw_grouped[:].rearrange("p q (c t) -> p q c t", t=PACK),
-                in_=lwT[:].rearrange("p (q t) c -> p q c t", t=PACK),
+                in_=lwT[:].rearrange("p (t q) c -> p q c t", t=PACK),
             )
             lw_codes = lw_pool.tile([P, BLOCK_PASSES * OUT_COLS], U32, name="lw_codes", align_bytes=64)
             lw_scales = lw_pool.tile([P, BLOCK_PASSES * OUT_COLS], U8, name="lw_scales", align_bytes=64)
@@ -204,13 +205,12 @@ def tile_softtreeensemble_pa_e_kernel(tc, x, W_words, W_scales, b, leaf_w, out):
             kids1 = prob_pool.tile([P, 2, 2, BATCH], F32, name="kids1")
             split(as_row(kids0), gates[1], kids1)
             quantised = []
-            for q in range(BLOCK_PASSES):
-                pair = slice(2 * q, 2 * q + 2)
+            for side in range(BLOCK_PASSES):
                 p6_grouped = leaf_pool.tile([P, BATCH * PACK], BF16, name="p6_grouped", align_bytes=64)
                 nc.vector.tensor_tensor(
-                    out=p6_grouped[:].rearrange("p (i a s) -> p i a s", a=2, s=2),
-                    in0=as_row(kids1)[:, pair, :].rearrange("p a i -> p i a").unsqueeze(3).to_broadcast([P, BATCH, 2, 2]),
-                    in1=gates[2][:, pair, :, :].rearrange("p a s i -> p i a s"),
+                    out=p6_grouped[:].rearrange("p (c i a) -> p c a i", i=RUN, a=PACK),
+                    in0=as_row(kids1).rearrange("p a (c i) -> p c a i", i=RUN),
+                    in1=gates[2][:, :, side, :].rearrange("p a (c i) -> p c a i", i=RUN),
                     op=MULT,
                 )
                 quantised.append(p6_grouped)

@@ -21,23 +21,13 @@ NODES = 2**DEPTH - 1
 LEAVES = 2**DEPTH
 HALVES = FEATURES // K_PASS
 BATCH_TILES = BATCH // P
-
-BLOCK_DEPTH = 3
-BLOCK_NODES = 2**BLOCK_DEPTH - 1
-BLOCK_OUTPUTS = 2**BLOCK_DEPTH
-BLOCKS = 1 + BLOCK_OUTPUTS
-BLOCK_PASSES = BLOCK_OUTPUTS // PACK
-RUN = 4
 LEAF_PASSES = LEAVES // PACK
-LOADS_AHEAD = 3
+RUN = 4
+QUAD = 4
+BLOCKS = 4
+PIN_VECTOR = False
 
 FLOPS = 2 * BATCH * FEATURES * NODES * TREES + 2 * BATCH * LEAVES * TREES * OUT_COLS
-
-
-def first_node(block, level):
-    if block == 0:
-        return 2**level - 1
-    return 2 ** (BLOCK_DEPTH + level) - 1 + (block - 1) * 2**level
 
 
 def tile_softtreeensemble_pa_e_kernel(tc, x, W_words, W_scales, b, leaf_w, out):
@@ -45,13 +35,15 @@ def tile_softtreeensemble_pa_e_kernel(tc, x, W_words, W_scales, b, leaf_w, out):
     with ExitStack() as ctx:
         const = ctx.enter_context(tc.tile_pool(name="const", bufs=1))
         x_pool = ctx.enter_context(tc.tile_pool(name="x_pool", bufs=BATCH_TILES))
-        w_pool = ctx.enter_context(tc.tile_pool(name="w_pool", bufs=LOADS_AHEAD + 1))
+        w_pool = ctx.enter_context(tc.tile_pool(name="w_pool", bufs=4))
         lw_pool = ctx.enter_context(tc.tile_pool(name="lw_pool", bufs=2))
-        gate_pool = ctx.enter_context(tc.tile_pool(name="gate_pool", bufs=2))
-        prob_pool = ctx.enter_context(tc.tile_pool(name="prob_pool", bufs=2))
-        leaf_pool = ctx.enter_context(tc.tile_pool(name="leaf_pool", bufs=2 * BLOCK_PASSES))
+        gate_pool = ctx.enter_context(tc.tile_pool(name="gate_pool", bufs=6))
+        kids_pool = ctx.enter_context(tc.tile_pool(name="kids_pool", bufs=3))
+        leaf_pool = ctx.enter_context(tc.tile_pool(name="leaf_pool", bufs=3))
         acc_pool = ctx.enter_context(tc.psum_pool(name="acc_pool", bufs=1))
         bank_pool = ctx.enter_context(tc.psum_pool(name="bank_pool", bufs=4))
+        if PIN_VECTOR:
+            ctx.enter_context(tc.manual_schedule(engines={mybir.EngineType.DVE}))
 
         ident_f32 = const.tile([P, P], F32)
         make_identity(nc, ident_f32[:])
@@ -82,30 +74,33 @@ def tile_softtreeensemble_pa_e_kernel(tc, x, W_words, W_scales, b, leaf_w, out):
                     in_=W_scales[groups, 4 * quad : 4 * quad + 4, :].rearrange("g r n -> r g n").bitcast(I32),
                 )
 
-        def load_block(block):
-            w_words = w_pool.tile([P, BLOCK_NODES, HALVES, TREES], U32, name="w_words", align_bytes=64)
-            for level in range(BLOCK_DEPTH):
-                count = 2**level
-                node = first_node(block, level)
-                if block == 1:
-                    load_scale_rows(node, count * BLOCK_OUTPUTS)
-                nc.sync.dma_start(
-                    out=w_words[:, count - 1 : 2 * count - 1, :, :].rearrange("p m h n -> p (m h) n").bitcast(I32),
-                    in_=W_words[HALVES * node : HALVES * (node + count)]
-                    .rearrange("g p n t -> p g (n t)")
-                    .bitcast(I32),
-                )
-            if block == 0:
-                return w_words, None
-            lw_sb = w_pool.tile([P, BLOCK_OUTPUTS, TREES], BF16, name="lw_sb")
-            first_leaf = (block - 1) * BLOCK_OUTPUTS
+        def load_words(tile_ap, node, count):
             nc.sync.dma_start(
-                out=lw_sb[:], in_=leaf_w[first_leaf : first_leaf + BLOCK_OUTPUTS].rearrange("j c t -> c j t")
+                out=tile_ap.rearrange("p m h n -> p (m h) n").bitcast(I32),
+                in_=W_words[HALVES * node : HALVES * (node + count)].rearrange("g p n t -> p g (n t)").bitcast(I32),
             )
-            return w_words, lw_sb
 
-        load_scale_rows(0, BLOCK_NODES)
-        loaded = [load_block(block) for block in range(LOADS_AHEAD)]
+        def load_quad(node):
+            w_words = w_pool.tile([P, QUAD, HALVES, TREES], U32, name="w_words", align_bytes=64)
+            load_words(w_words[:], node, QUAD)
+            return w_words
+
+        def load_leaf_weights(group):
+            lw_sb = lw_pool.tile([P, 2 * QUAD, TREES], BF16, name="lw_sb", bufs=3)
+            nc.sync.dma_start(
+                out=lw_sb[:], in_=leaf_w[8 * group : 8 * group + 8].rearrange("j c t -> c j t")
+            )
+            return lw_sb
+
+        load_scale_rows(0, 15)
+        w_head = const.tile([P, 7, HALVES, TREES], U32, align_bytes=64)
+        load_words(w_head[:, 0:1, :, :], 0, 1)
+        load_words(w_head[:, 1:3, :, :], 1, 2)
+        load_words(w_head[:, 3:7, :, :], 3, 4)
+        w_l3 = [load_quad(7), load_quad(11)]
+        load_scale_rows(15, 16)
+        w_l4 = {0: load_quad(15)}
+        load_scale_rows(31, 32)
 
         x_codes = const.tile([P, HALVES, BATCH], U32, align_bytes=64)
         x_scales = const.tile([P, HALVES, BATCH], U8, align_bytes=64)
@@ -117,7 +112,7 @@ def tile_softtreeensemble_pa_e_kernel(tc, x, W_words, W_scales, b, leaf_w, out):
                     nc.tensor.transpose(
                         xT[:, h, u, :], x_words[:, 256 * h + u : 256 * (h + 1) : 2], ident_f32[:]
                     )
-            x_grouped = x_pool.tile([P, HALVES, P * PACK], BF16, name="x_grouped", align_bytes=64)
+            x_grouped = x_pool.tile([P, HALVES, P * PACK], BF16, name="x_grouped", align_bytes=64, bufs=2)
             grouped_words = x_grouped[:].bitcast(F32).rearrange("p h (i u) -> p h i u", u=2)
             if bt % 2 == 0:
                 nc.vector.tensor_copy(out=grouped_words, in_=xT[:].rearrange("p h u i -> p h i u"))
@@ -136,123 +131,193 @@ def tile_softtreeensemble_pa_e_kernel(tc, x, W_words, W_scales, b, leaf_w, out):
         bias_negated = const.tile([P, P], F32)
         nc.vector.tensor_scalar_mul(out=bias_negated[:], in0=bT[:], scalar1=-1.0)
 
-        def gate_block(block, w_words):
-            gates = []
-            for level in range(BLOCK_DEPTH):
-                count = 2**level
-                both = (block == 0 and level == 0) or (block > 0 and level == BLOCK_DEPTH - 1)
-                gate = gate_pool.tile([P, count, 2 if both else 1, BATCH], F32, name="gate%d" % level)
-                for j in range(count):
-                    node = first_node(block, level) + j
-                    z = bank_pool.tile([P, BATCH], F32, tag="bank")
-                    for h in range(HALVES):
-                        nc.tensor.matmul_mx(
-                            out=z[:],
-                            lhsT=w_words[:, count - 1 + j, h, :].bitcast(FP8X4),
-                            lhsT_scale=w_planes[:, HALVES * node + h, :],
-                            rhs=x_codes[:, h, :].bitcast(FP8X4),
-                            rhs_scale=x_scales[:, h, :],
-                            start=(h == 0),
-                            stop=(h == HALVES - 1),
-                        )
-                    nc.scalar.activation(
-                        out=gate[:, j, 0, :], in_=z[:], func=SIGMOID, bias=bias[:, node : node + 1], scale=1.0
-                    )
-                    if both:
-                        nc.scalar.activation(
-                            out=gate[:, j, 1, :],
-                            in_=z[:],
-                            func=SIGMOID,
-                            bias=bias_negated[:, node : node + 1],
-                            scale=-1.0,
-                        )
-                gates.append(gate)
-            return gates
+        def node_z(node, words, slot):
+            z = bank_pool.tile([P, BATCH], F32, tag="bank")
+            for h in range(HALVES):
+                nc.tensor.matmul_mx(
+                    out=z[:],
+                    lhsT=words[:, slot, h, :].bitcast(FP8X4),
+                    lhsT_scale=w_planes[:, HALVES * node + h, :],
+                    rhs=x_codes[:, h, :].bitcast(FP8X4),
+                    rhs_scale=x_scales[:, h, :],
+                    start=(h == 0),
+                    stop=(h == HALVES - 1),
+                )
+            return z
 
-        def quantise_leaf_weights(lw_sb):
-            lwT = bank_pool.tile([P, BLOCK_OUTPUTS, OUT_COLS], BF16, tag="bank")
-            for j in range(BLOCK_OUTPUTS):
+        def left_gate(dst, z, node):
+            nc.scalar.activation(out=dst, in_=z[:], func=SIGMOID, bias=bias[:, node : node + 1], scale=1.0)
+
+        def right_gate(dst, z, node):
+            nc.scalar.activation(
+                out=dst, in_=z[:], func=SIGMOID, bias=bias_negated[:, node : node + 1], scale=-1.0
+            )
+
+        def gate_tile():
+            return gate_pool.tile([P, QUAD, BATCH], F32, name="gate")
+
+        def left_gates(node, count, words, first_slot):
+            gate = gate_tile()
+            for j in range(count):
+                left_gate(gate[:, j, :], node_z(node + j, words, first_slot + j), node + j)
+            return gate
+
+        def both_gates(node, words):
+            left_tile = gate_tile()
+            right_tile = gate_tile()
+            for j in range(QUAD):
+                z = node_z(node + j, words, j)
+                left_gate(left_tile[:, j, :], z, node + j)
+                right_gate(right_tile[:, j, :], z, node + j)
+            return left_tile, right_tile
+
+        def transpose_leaf_weights(lw_sb, lw_grouped, half):
+            lwT = bank_pool.tile([P, 2 * QUAD, OUT_COLS], BF16, tag="bank")
+            for j in range(2 * QUAD):
                 nc.tensor.transpose(lwT[:, j, :], lw_sb[:, j, :], ident_bf16[:])
-            lw_grouped = lw_pool.tile([P, BLOCK_PASSES, OUT_COLS * PACK], BF16, name="lw_grouped", align_bytes=64)
             nc.scalar.copy(
-                out=lw_grouped[:].rearrange("p q (c t) -> p q c t", t=PACK),
+                out=lw_grouped[:, 2 * half : 2 * half + 2, :].rearrange("p q (c t) -> p q c t", t=PACK),
                 in_=lwT[:].rearrange("p (t q) c -> p q c t", t=PACK),
             )
-            lw_codes = lw_pool.tile([P, BLOCK_PASSES * OUT_COLS], U32, name="lw_codes", align_bytes=64)
-            lw_scales = lw_pool.tile([P, BLOCK_PASSES * OUT_COLS], U8, name="lw_scales", align_bytes=64)
+
+        def group_leaf_weights(raw):
+            lw_grouped = lw_pool.tile([P, 4, OUT_COLS * PACK], BF16, name="lw_grouped", align_bytes=64)
+            for half in range(2):
+                transpose_leaf_weights(raw[half], lw_grouped, half)
+            return lw_grouped
+
+        def quantise_leaf_weights(lw_grouped):
+            lw_codes = lw_pool.tile([P, 4 * OUT_COLS], U32, name="lw_codes", align_bytes=64)
+            lw_scales = lw_pool.tile([P, 4 * OUT_COLS], U8, name="lw_scales", align_bytes=64)
             nc.vector.quantize_mx(
                 out=lw_codes[:].bitcast(FP8X4), scales=lw_scales[:], in_=lw_grouped[:].rearrange("p q n -> p (q n)")
             )
             return lw_codes, lw_scales
 
-        def split(parents, gate, kids):
-            nc.vector.tensor_mul(out=kids[:, :, 0, :], in0=parents, in1=gate[:, :, 0, :])
-            nc.vector.tensor_sub(out=kids[:, :, 1, :], in0=parents, in1=kids[:, :, 0, :])
+        def kids_tile(count):
+            return kids_pool.tile([P, count, 2, BATCH], F32, name="kids")
 
         def as_row(kids):
             return kids[:].rearrange("p j s i -> p (j s) i")
 
-        level3 = const.tile([P, BLOCK_OUTPUTS // 2, 2, BATCH], F32)
+        def lefts(parents, gate, kids, nodes):
+            nc.vector.tensor_mul(out=kids[:, nodes, 0, :], in0=parents, in1=gate[:, nodes, :])
 
-        def top_block(gates):
-            kids1 = prob_pool.tile([P, 2, 2, BATCH], F32, name="kids1")
-            split(as_row(gates[0]), gates[1], kids1)
-            split(as_row(kids1), gates[2], level3)
+        def rights(parents, kids, nodes):
+            nc.vector.tensor_sub(out=kids[:, nodes, 1, :], in0=parents, in1=kids[:, nodes, 0, :])
 
-        def leaf_block(block, gates):
-            kids0 = prob_pool.tile([P, 1, 2, BATCH], F32, name="kids0")
-            split(as_row(level3)[:, block - 1 : block, :], gates[0], kids0)
-            kids1 = prob_pool.tile([P, 2, 2, BATCH], F32, name="kids1")
-            split(as_row(kids0), gates[1], kids1)
-            quantised = []
-            for side in range(BLOCK_PASSES):
-                p6_grouped = leaf_pool.tile([P, BATCH * PACK], BF16, name="p6_grouped", align_bytes=64)
-                nc.vector.tensor_tensor(
-                    out=p6_grouped[:].rearrange("p (c i a) -> p c a i", i=RUN, a=PACK),
-                    in0=as_row(kids1).rearrange("p a (c i) -> p c a i", i=RUN),
-                    in1=gates[2][:, :, side, :].rearrange("p a (c i) -> p c a i", i=RUN),
-                    op=MULT,
-                )
-                quantised.append(p6_grouped)
-            words = []
-            for q in range(BLOCK_PASSES):
-                p6_codes = leaf_pool.tile([P, BATCH], U32, name="p6_codes", align_bytes=64)
-                p6_scales = leaf_pool.tile([P, BATCH], U8, name="p6_scales", align_bytes=64)
-                nc.vector.quantize_mx(out=p6_codes[:].bitcast(FP8X4), scales=p6_scales[:], in_=quantised[q][:])
-                words.append((p6_codes, p6_scales))
-            return words
+        def leaf_products(parents, gate):
+            p6_grouped = leaf_pool.tile([P, BATCH * PACK], BF16, name="p6_grouped", align_bytes=64)
+            nc.vector.tensor_tensor(
+                out=p6_grouped[:].rearrange("p (c i a) -> p c a i", i=RUN, a=PACK),
+                in0=parents.rearrange("p a (c i) -> p c a i", i=RUN),
+                in1=gate[:].rearrange("p a (c i) -> p c a i", i=RUN),
+                op=MULT,
+            )
+            return p6_grouped
 
         acc = [acc_pool.tile([P, BATCH], F32, name="acc%d" % bt) for bt in range(BATCH_TILES)]
 
-        def second_matmul(block, words, lw_codes, lw_scales):
-            for q in range(BLOCK_PASSES):
-                leaf_pass = (block - 1) * BLOCK_PASSES + q
-                p6_codes, p6_scales = words[q]
-                out_cols = slice(q * OUT_COLS, (q + 1) * OUT_COLS)
-                for bt in range(BATCH_TILES):
-                    rows = slice(bt * P, (bt + 1) * P)
-                    nc.tensor.matmul_mx(
-                        out=acc[bt][:, :OUT_COLS],
-                        lhsT=p6_codes[:, rows].bitcast(FP8X4),
-                        lhsT_scale=p6_scales[:, rows],
-                        rhs=lw_codes[:, out_cols].bitcast(FP8X4),
-                        rhs_scale=lw_scales[:, out_cols],
-                        start=(leaf_pass == 0),
-                        stop=(leaf_pass == LEAF_PASSES - 1),
-                    )
+        def quantise_and_contract(leaf_pass, p6_grouped, lw):
+            p6_codes = leaf_pool.tile([P, BATCH], U32, name="p6_codes", align_bytes=64)
+            p6_scales = leaf_pool.tile([P, BATCH], U8, name="p6_scales", align_bytes=64)
+            nc.vector.quantize_mx(out=p6_codes[:].bitcast(FP8X4), scales=p6_scales[:], in_=p6_grouped[:])
+            out_cols = slice((leaf_pass % 4) * OUT_COLS, (leaf_pass % 4 + 1) * OUT_COLS)
+            for bt in range(BATCH_TILES):
+                rows = slice(bt * P, (bt + 1) * P)
+                nc.tensor.matmul_mx(
+                    out=acc[bt][:, :OUT_COLS],
+                    lhsT=p6_codes[:, rows].bitcast(FP8X4),
+                    lhsT_scale=p6_scales[:, rows],
+                    rhs=lw[0][:, out_cols].bitcast(FP8X4),
+                    rhs_scale=lw[1][:, out_cols],
+                    start=(leaf_pass == 0),
+                    stop=(leaf_pass == LEAF_PASSES - 1),
+                )
 
-        gates = gate_block(0, loaded[0][0])
+        p1 = gate_pool.tile([P, 2, BATCH], F32, name="gate")
+        g1 = gate_pool.tile([P, 2, BATCH], F32, name="gate")
+        z0 = node_z(0, w_head, 0)
+        left_gate(p1[:, 0, :], z0, 0)
+        left_gate(g1[:, 0, :], node_z(1, w_head, 1), 1)
+        right_gate(p1[:, 1, :], z0, 0)
+        left_gate(g1[:, 1, :], node_z(2, w_head, 2), 2)
+        g2 = left_gates(3, 4, w_head, 3)
+
+        kids2 = kids_tile(2)
+        for j in range(2):
+            lefts(p1[:, j : j + 1, :], g1, kids2, slice(j, j + 1))
+        for j in range(2):
+            rights(p1[:, j : j + 1, :], kids2, slice(j, j + 1))
+
+        g3 = [left_gates(7 + 4 * k, 4, w_l3[k], 0) for k in range(2)]
+        w_l5 = {0: load_quad(31), 1: load_quad(35)}
+        lw_raw = {0: [load_leaf_weights(0), load_leaf_weights(1)]}
+
+        kids3 = kids_tile(4)
+        for k in range(2):
+            lefts(as_row(kids2)[:, 2 * k : 2 * k + 2, :], g2, kids3, slice(2 * k, 2 * k + 2))
+        for k in range(2):
+            rights(as_row(kids2)[:, 2 * k : 2 * k + 2, :], kids3, slice(2 * k, 2 * k + 2))
+
+        g4 = {0: left_gates(15, 4, w_l4[0], 0)}
+        w_l4[1] = load_quad(19)
+        lw_grouped = {0: group_leaf_weights(lw_raw[0])}
+
+        kids4 = [const.tile([P, QUAD, 2, BATCH], F32, name="kids4_%d" % k) for k in range(2)]
+        for k in range(2):
+            lefts(as_row(kids3)[:, 4 * k : 4 * k + 4, :], g3[k], kids4[k], slice(0, 4))
+        for k in range(2):
+            rights(as_row(kids3)[:, 4 * k : 4 * k + 4, :], kids4[k], slice(0, 4))
+
+        def level4_parents(block):
+            return as_row(kids4[block // 2])[:, 4 * (block % 2) : 4 * (block % 2) + 4, :]
+
+        g5 = {}
+        kids5 = {}
+        lw = {}
+
+        def make_level5_gates(block, half):
+            g5[(block, half)] = both_gates(31 + 8 * block + 4 * half, w_l5[2 * block + half])
+
+        make_level5_gates(0, 0)
+        kids5[0] = kids_tile(4)
+        lefts(level4_parents(0), g4[0], kids5[0], slice(0, 4))
+        lw[0] = quantise_leaf_weights(lw_grouped[0])
+        rights(level4_parents(0), kids5[0], slice(0, 4))
+
+        waiting = None
         for block in range(BLOCKS):
-            if block + LOADS_AHEAD < BLOCKS:
-                loaded.append(load_block(block + LOADS_AHEAD))
-            if block + 1 < BLOCKS:
-                next_gates = gate_block(block + 1, loaded[block + 1][0])
-                next_lw = quantise_leaf_weights(loaded[block + 1][1])
-            if block == 0:
-                top_block(gates)
-            else:
-                second_matmul(block, leaf_block(block, gates), lw[0], lw[1])
-            gates, lw = next_gates, next_lw
+            following = block + 1
+            for q in range(4):
+                half, side = q // 2, q % 2
+                if q == 0:
+                    make_level5_gates(block, 1)
+                    if following < BLOCKS:
+                        w_l5[2 * following] = load_quad(31 + 8 * following)
+                        w_l5[2 * following + 1] = load_quad(35 + 8 * following)
+                        lw_raw[following] = [load_leaf_weights(2 * following), load_leaf_weights(2 * following + 1)]
+                        g4[following] = left_gates(15 + 4 * following, 4, w_l4[following], 0)
+                        if following + 1 < BLOCKS:
+                            w_l4[following + 1] = load_quad(15 + 4 * (following + 1))
+                if q == 1 and following < BLOCKS:
+                    lw_grouped[following] = group_leaf_weights(lw_raw[following])
+                if q == 2 and following < BLOCKS:
+                    make_level5_gates(following, 0)
+
+                products = leaf_products(as_row(kids5[block])[:, 4 * half : 4 * half + 4, :], g5[(block, half)][side])
+                if waiting is not None:
+                    quantise_and_contract(waiting[0], waiting[1], lw[waiting[0] // 4])
+                waiting = (4 * block + q, products)
+                if following < BLOCKS:
+                    if q == 1:
+                        kids5[following] = kids_tile(4)
+                        lefts(level4_parents(following), g4[following], kids5[following], slice(0, 4))
+                    if q == 2:
+                        rights(level4_parents(following), kids5[following], slice(0, 4))
+                    if q == 3:
+                        lw[following] = quantise_leaf_weights(lw_grouped[following])
+        quantise_and_contract(waiting[0], waiting[1], lw[waiting[0] // 4])
 
         out_sb = const.tile([P, BATCH_TILES, OUT_COLS], F32)
         for bt in range(BATCH_TILES):

@@ -25,7 +25,7 @@ LEAF_PASSES = LEAVES // PACK
 RUN = 4
 QUAD = 4
 BLOCKS = 4
-PIN_VECTOR = False
+PIN_VECTOR = True
 
 FLOPS = 2 * BATCH * FEATURES * NODES * TREES + 2 * BATCH * LEAVES * TREES * OUT_COLS
 
@@ -39,7 +39,7 @@ def tile_softtreeensemble_pa_e_kernel(tc, x, W_words, W_scales, b, leaf_w, out):
         lw_pool = ctx.enter_context(tc.tile_pool(name="lw_pool", bufs=2))
         gate_pool = ctx.enter_context(tc.tile_pool(name="gate_pool", bufs=6))
         kids_pool = ctx.enter_context(tc.tile_pool(name="kids_pool", bufs=3))
-        leaf_pool = ctx.enter_context(tc.tile_pool(name="leaf_pool", bufs=3))
+        leaf_pool = ctx.enter_context(tc.tile_pool(name="leaf_pool", bufs=2))
         acc_pool = ctx.enter_context(tc.psum_pool(name="acc_pool", bufs=1))
         bank_pool = ctx.enter_context(tc.psum_pool(name="bank_pool", bufs=4))
         if PIN_VECTOR:
@@ -206,34 +206,36 @@ def tile_softtreeensemble_pa_e_kernel(tc, x, W_words, W_scales, b, leaf_w, out):
         def rights(parents, kids, nodes):
             nc.vector.tensor_sub(out=kids[:, nodes, 1, :], in0=parents, in1=kids[:, nodes, 0, :])
 
-        def leaf_products(parents, gate):
-            p6_grouped = leaf_pool.tile([P, BATCH * PACK], BF16, name="p6_grouped", align_bytes=64)
+        def leaf_products(p6_pair, side, parents, gate):
             nc.vector.tensor_tensor(
-                out=p6_grouped[:].rearrange("p (c i a) -> p c a i", i=RUN, a=PACK),
+                out=p6_pair[:, side, :].rearrange("p (c i a) -> p c a i", i=RUN, a=PACK),
                 in0=parents.rearrange("p a (c i) -> p c a i", i=RUN),
                 in1=gate[:].rearrange("p a (c i) -> p c a i", i=RUN),
                 op=MULT,
             )
-            return p6_grouped
 
         acc = [acc_pool.tile([P, BATCH], F32, name="acc%d" % bt) for bt in range(BATCH_TILES)]
 
-        def quantise_and_contract(leaf_pass, p6_grouped, lw):
-            p6_codes = leaf_pool.tile([P, BATCH], U32, name="p6_codes", align_bytes=64)
-            p6_scales = leaf_pool.tile([P, BATCH], U8, name="p6_scales", align_bytes=64)
-            nc.vector.quantize_mx(out=p6_codes[:].bitcast(FP8X4), scales=p6_scales[:], in_=p6_grouped[:])
-            out_cols = slice((leaf_pass % 4) * OUT_COLS, (leaf_pass % 4 + 1) * OUT_COLS)
-            for bt in range(BATCH_TILES):
-                rows = slice(bt * P, (bt + 1) * P)
-                nc.tensor.matmul_mx(
-                    out=acc[bt][:, :OUT_COLS],
-                    lhsT=p6_codes[:, rows].bitcast(FP8X4),
-                    lhsT_scale=p6_scales[:, rows],
-                    rhs=lw[0][:, out_cols].bitcast(FP8X4),
-                    rhs_scale=lw[1][:, out_cols],
-                    start=(leaf_pass == 0),
-                    stop=(leaf_pass == LEAF_PASSES - 1),
-                )
+        def quantise_and_contract(first_pass, p6_pair, lw):
+            p6_codes = leaf_pool.tile([P, 2 * BATCH], U32, name="p6_codes", align_bytes=64)
+            p6_scales = leaf_pool.tile([P, 2 * BATCH], U8, name="p6_scales", align_bytes=64)
+            nc.vector.quantize_mx(
+                out=p6_codes[:].bitcast(FP8X4), scales=p6_scales[:], in_=p6_pair[:].rearrange("p s n -> p (s n)")
+            )
+            for side in range(2):
+                leaf_pass = first_pass + side
+                out_cols = slice((leaf_pass % 4) * OUT_COLS, (leaf_pass % 4 + 1) * OUT_COLS)
+                for bt in range(BATCH_TILES):
+                    rows = slice(side * BATCH + bt * P, side * BATCH + (bt + 1) * P)
+                    nc.tensor.matmul_mx(
+                        out=acc[bt][:, :OUT_COLS],
+                        lhsT=p6_codes[:, rows].bitcast(FP8X4),
+                        lhsT_scale=p6_scales[:, rows],
+                        rhs=lw[0][:, out_cols].bitcast(FP8X4),
+                        rhs_scale=lw[1][:, out_cols],
+                        start=(leaf_pass == 0),
+                        stop=(leaf_pass == LEAF_PASSES - 1),
+                    )
 
         p1 = gate_pool.tile([P, 2, BATCH], F32, name="gate")
         g1 = gate_pool.tile([P, 2, BATCH], F32, name="gate")
@@ -262,7 +264,6 @@ def tile_softtreeensemble_pa_e_kernel(tc, x, W_words, W_scales, b, leaf_w, out):
 
         g4 = {0: left_gates(15, 4, w_l4[0], 0)}
         w_l4[1] = load_quad(19)
-        lw_grouped = {0: group_leaf_weights(lw_raw[0])}
 
         kids4 = [const.tile([P, QUAD, 2, BATCH], F32, name="kids4_%d" % k) for k in range(2)]
         for k in range(2):
@@ -275,49 +276,47 @@ def tile_softtreeensemble_pa_e_kernel(tc, x, W_words, W_scales, b, leaf_w, out):
 
         g5 = {}
         kids5 = {}
-        lw = {}
 
         def make_level5_gates(block, half):
             g5[(block, half)] = both_gates(31 + 8 * block + 4 * half, w_l5[2 * block + half])
 
         make_level5_gates(0, 0)
         kids5[0] = kids_tile(4)
-        lefts(level4_parents(0), g4[0], kids5[0], slice(0, 4))
-        lw[0] = quantise_leaf_weights(lw_grouped[0])
-        rights(level4_parents(0), kids5[0], slice(0, 4))
+        for k in range(2):
+            lefts(level4_parents(0)[:, 2 * k : 2 * k + 2, :], g4[0], kids5[0], slice(2 * k, 2 * k + 2))
+        for k in range(2):
+            rights(level4_parents(0)[:, 2 * k : 2 * k + 2, :], kids5[0], slice(2 * k, 2 * k + 2))
 
-        waiting = None
+        def pair_products(block, half):
+            p6_pair = leaf_pool.tile([P, 2, BATCH * PACK], BF16, name="p6_pair", align_bytes=64)
+            for side in range(2):
+                leaf_products(
+                    p6_pair, side, as_row(kids5[block])[:, 4 * half : 4 * half + 4, :], g5[(block, half)][side]
+                )
+            return p6_pair
+
         for block in range(BLOCKS):
             following = block + 1
-            for q in range(4):
-                half, side = q // 2, q % 2
-                if q == 0:
-                    make_level5_gates(block, 1)
-                    if following < BLOCKS:
-                        w_l5[2 * following] = load_quad(31 + 8 * following)
-                        w_l5[2 * following + 1] = load_quad(35 + 8 * following)
-                        lw_raw[following] = [load_leaf_weights(2 * following), load_leaf_weights(2 * following + 1)]
-                        g4[following] = left_gates(15 + 4 * following, 4, w_l4[following], 0)
-                        if following + 1 < BLOCKS:
-                            w_l4[following + 1] = load_quad(15 + 4 * (following + 1))
-                if q == 1 and following < BLOCKS:
-                    lw_grouped[following] = group_leaf_weights(lw_raw[following])
-                if q == 2 and following < BLOCKS:
-                    make_level5_gates(following, 0)
-
-                products = leaf_products(as_row(kids5[block])[:, 4 * half : 4 * half + 4, :], g5[(block, half)][side])
-                if waiting is not None:
-                    quantise_and_contract(waiting[0], waiting[1], lw[waiting[0] // 4])
-                waiting = (4 * block + q, products)
-                if following < BLOCKS:
-                    if q == 1:
-                        kids5[following] = kids_tile(4)
-                        lefts(level4_parents(following), g4[following], kids5[following], slice(0, 4))
-                    if q == 2:
-                        rights(level4_parents(following), kids5[following], slice(0, 4))
-                    if q == 3:
-                        lw[following] = quantise_leaf_weights(lw_grouped[following])
-        quantise_and_contract(waiting[0], waiting[1], lw[waiting[0] // 4])
+            make_level5_gates(block, 1)
+            if following < BLOCKS:
+                w_l5[2 * following] = load_quad(31 + 8 * following)
+                w_l5[2 * following + 1] = load_quad(35 + 8 * following)
+                lw_raw[following] = [load_leaf_weights(2 * following), load_leaf_weights(2 * following + 1)]
+                g4[following] = left_gates(15 + 4 * following, 4, w_l4[following], 0)
+                if following + 1 < BLOCKS:
+                    w_l4[following + 1] = load_quad(15 + 4 * (following + 1))
+            first_pair = pair_products(block, 0)
+            lw_grouped = group_leaf_weights(lw_raw[block])
+            if following < BLOCKS:
+                kids5[following] = kids_tile(4)
+                lefts(level4_parents(following), g4[following], kids5[following], slice(0, 4))
+                make_level5_gates(following, 0)
+            second_pair = pair_products(block, 1)
+            if following < BLOCKS:
+                rights(level4_parents(following), kids5[following], slice(0, 4))
+            lw = quantise_leaf_weights(lw_grouped)
+            quantise_and_contract(4 * block, first_pair, lw)
+            quantise_and_contract(4 * block + 2, second_pair, lw)
 
         out_sb = const.tile([P, BATCH_TILES, OUT_COLS], F32)
         for bt in range(BATCH_TILES):

@@ -26,6 +26,8 @@ RUN = 4
 QUAD = 4
 BLOCKS = 4
 PIN_VECTOR = True
+WARM_MATMULS = 4
+HALF = BATCH // 2
 
 FLOPS = 2 * BATCH * FEATURES * NODES * TREES + 2 * BATCH * LEAVES * TREES * OUT_COLS
 
@@ -49,6 +51,11 @@ def tile_softtreeensemble_pa_e_kernel(tc, x, W_words, W_scales, b, leaf_w, out):
         make_identity(nc, ident_f32[:])
         ident_bf16 = const.tile([P, P], BF16)
         make_identity(nc, ident_bf16[:])
+        zeros = const.tile([P, BATCH], BF16)
+        nc.vector.memset(zeros[:], 0.0)
+        idle_bank = bank_pool.tile([P, BATCH], F32, tag="bank")
+        for k in range(WARM_MATMULS):
+            nc.tensor.matmul(out=idle_bank[:], lhsT=zeros[:, :P], rhs=zeros[:], start=True, stop=True)
         warm = const.tile([P, 1], F32)
         nc.vector.memset(warm[:], 0.0)
         nc.scalar.activation(out=warm[:], in_=warm[:], func=SIGMOID)
@@ -131,15 +138,17 @@ def tile_softtreeensemble_pa_e_kernel(tc, x, W_words, W_scales, b, leaf_w, out):
         bias_negated = const.tile([P, P], F32)
         nc.vector.tensor_scalar_mul(out=bias_negated[:], in0=bT[:], scalar1=-1.0)
 
-        def node_z(node, words, slot):
-            z = bank_pool.tile([P, BATCH], F32, tag="bank")
+        whole = slice(0, BATCH)
+
+        def node_z(node, words, slot, cols=whole):
+            z = bank_pool.tile([P, cols.stop - cols.start], F32, tag="bank")
             for h in range(HALVES):
                 nc.tensor.matmul_mx(
                     out=z[:],
                     lhsT=words[:, slot, h, :].bitcast(FP8X4),
                     lhsT_scale=w_planes[:, HALVES * node + h, :],
-                    rhs=x_codes[:, h, :].bitcast(FP8X4),
-                    rhs_scale=x_scales[:, h, :],
+                    rhs=x_codes[:, h, cols].bitcast(FP8X4),
+                    rhs_scale=x_scales[:, h, cols],
                     start=(h == 0),
                     stop=(h == HALVES - 1),
                 )
@@ -200,11 +209,11 @@ def tile_softtreeensemble_pa_e_kernel(tc, x, W_words, W_scales, b, leaf_w, out):
         def as_row(kids):
             return kids[:].rearrange("p j s i -> p (j s) i")
 
-        def lefts(parents, gate, kids, nodes):
-            nc.vector.tensor_mul(out=kids[:, nodes, 0, :], in0=parents, in1=gate[:, nodes, :])
+        def lefts(parents, gate, kids, nodes, cols=whole):
+            nc.vector.tensor_mul(out=kids[:, nodes, 0, cols], in0=parents, in1=gate[:, nodes, cols])
 
-        def rights(parents, kids, nodes):
-            nc.vector.tensor_sub(out=kids[:, nodes, 1, :], in0=parents, in1=kids[:, nodes, 0, :])
+        def rights(parents, kids, nodes, cols=whole):
+            nc.vector.tensor_sub(out=kids[:, nodes, 1, cols], in0=parents, in1=kids[:, nodes, 0, cols])
 
         def leaf_products(p6_pair, side, parents, gate):
             nc.vector.tensor_tensor(
@@ -239,28 +248,45 @@ def tile_softtreeensemble_pa_e_kernel(tc, x, W_words, W_scales, b, leaf_w, out):
 
         p1 = gate_pool.tile([P, 2, BATCH], F32, name="gate")
         g1 = gate_pool.tile([P, 2, BATCH], F32, name="gate")
-        z0 = node_z(0, w_head, 0)
-        left_gate(p1[:, 0, :], z0, 0)
-        left_gate(g1[:, 0, :], node_z(1, w_head, 1), 1)
-        right_gate(p1[:, 1, :], z0, 0)
-        left_gate(g1[:, 1, :], node_z(2, w_head, 2), 2)
-        g2 = left_gates(3, 4, w_head, 3)
-
+        g2 = gate_tile()
         kids2 = kids_tile(2)
-        for j in range(2):
-            lefts(p1[:, j : j + 1, :], g1, kids2, slice(j, j + 1))
-        for j in range(2):
-            rights(p1[:, j : j + 1, :], kids2, slice(j, j + 1))
+        kids3 = kids_tile(4)
+        halves = [slice(0, HALF), slice(HALF, BATCH)]
 
+        def first_gates(cols):
+            z0 = node_z(0, w_head, 0, cols)
+            left_gate(p1[:, 0, cols], z0, 0)
+            left_gate(g1[:, 0, cols], node_z(1, w_head, 1, cols), 1)
+            right_gate(p1[:, 1, cols], z0, 0)
+            left_gate(g1[:, 1, cols], node_z(2, w_head, 2, cols), 2)
+
+        def level2_gates(cols):
+            for j in range(4):
+                left_gate(g2[:, j, cols], node_z(3 + j, w_head, 3 + j, cols), 3 + j)
+
+        def level1_products(cols):
+            for j in range(2):
+                lefts(p1[:, j : j + 1, cols], g1, kids2, slice(j, j + 1), cols)
+            for j in range(2):
+                rights(p1[:, j : j + 1, cols], kids2, slice(j, j + 1), cols)
+
+        def level2_products(cols):
+            for k in range(2):
+                lefts(as_row(kids2)[:, 2 * k : 2 * k + 2, cols], g2, kids3, slice(2 * k, 2 * k + 2), cols)
+            for k in range(2):
+                rights(as_row(kids2)[:, 2 * k : 2 * k + 2, cols], kids3, slice(2 * k, 2 * k + 2), cols)
+
+        first_gates(halves[0])
+        first_gates(halves[1])
+        level1_products(halves[0])
+        level2_gates(halves[0])
+        level1_products(halves[1])
+        level2_gates(halves[1])
         g3 = [left_gates(7 + 4 * k, 4, w_l3[k], 0) for k in range(2)]
         w_l5 = {0: load_quad(31), 1: load_quad(35)}
         lw_raw = {0: [load_leaf_weights(0), load_leaf_weights(1)]}
-
-        kids3 = kids_tile(4)
-        for k in range(2):
-            lefts(as_row(kids2)[:, 2 * k : 2 * k + 2, :], g2, kids3, slice(2 * k, 2 * k + 2))
-        for k in range(2):
-            rights(as_row(kids2)[:, 2 * k : 2 * k + 2, :], kids3, slice(2 * k, 2 * k + 2))
+        level2_products(halves[0])
+        level2_products(halves[1])
 
         g4 = {0: left_gates(15, 4, w_l4[0], 0)}
         w_l4[1] = load_quad(19)

@@ -45,12 +45,22 @@ def tile_softtreeensemble_pa_e_kernel(tc, x, W_words, W_scales, b, leaf_w, out):
         acc_pool = ctx.enter_context(tc.psum_pool(name="acc_pool", bufs=1))
         bank_pool = ctx.enter_context(tc.psum_pool(name="bank_pool", bufs=4))
         if PIN_VECTOR:
-            ctx.enter_context(tc.manual_schedule(engines={mybir.EngineType.DVE}))
+            ctx.enter_context(tc.manual_schedule(engines={mybir.EngineType.DVE, mybir.EngineType.SP}))
 
-        ident_f32 = const.tile([P, P], F32)
-        make_identity(nc, ident_f32[:])
-        ident_bf16 = const.tile([P, P], BF16)
-        make_identity(nc, ident_bf16[:])
+        w_planes = const.tile([P, HALVES * NODES, TREES], U8, align_bytes=64)
+
+        def zero_scale_planes(node, count):
+            nc.vector.memset(w_planes[:, HALVES * node : HALVES * (node + count), :].bitcast(I32), 0)
+
+        def load_scale_rows(node, count):
+            groups = slice(HALVES * node, HALVES * (node + count))
+            for quad in range(4):
+                nc.sync.dma_start(
+                    out=w_planes[32 * quad : 32 * quad + 4, groups, :].bitcast(I32),
+                    in_=W_scales[groups, 4 * quad : 4 * quad + 4, :].rearrange("g r n -> r g n").bitcast(I32),
+                )
+
+        zero_scale_planes(0, 7)
         zeros = const.tile([P, BATCH], BF16)
         nc.vector.memset(zeros[:], 0.0)
         idle_bank = bank_pool.tile([P, BATCH], F32, tag="bank")
@@ -59,27 +69,21 @@ def tile_softtreeensemble_pa_e_kernel(tc, x, W_words, W_scales, b, leaf_w, out):
         warm = const.tile([P, 1], F32)
         nc.vector.memset(warm[:], 0.0)
         nc.scalar.activation(out=warm[:], in_=warm[:], func=SIGMOID)
+        zero_scale_planes(7, 8)
+        zero_scale_planes(15, 48)
 
-        x_rows = []
-        for bt in range(BATCH_TILES):
+        ident_f32 = const.tile([P, P], F32)
+        make_identity(nc, ident_f32[:])
+        b_rows = const.tile([P, P], BF16)
+        nc.gpsimd.memset(b_rows[:], 0.0)
+        nc.gpsimd.dma_start(out=b_rows[:NODES, :], in_=b)
+        ident_bf16 = const.tile([P, P], BF16)
+        make_identity(nc, ident_bf16[:])
+
+        def load_x(bt):
             x_sb = x_pool.tile([P, FEATURES], BF16, name="x_sb")
             nc.sync.dma_start(out=x_sb[:], in_=x[bt * P : (bt + 1) * P, :])
-            x_rows.append(x_sb)
-
-        b_rows = const.tile([P, P], BF16)
-        nc.vector.memset(b_rows[:], 0.0)
-        nc.scalar.dma_start(out=b_rows[:NODES, :], in_=b)
-
-        w_planes = const.tile([P, HALVES * NODES, TREES], U8, align_bytes=64)
-
-        def load_scale_rows(node, count):
-            groups = slice(HALVES * node, HALVES * (node + count))
-            nc.vector.memset(w_planes[:, groups, :].bitcast(I32), 0)
-            for quad in range(4):
-                nc.sync.dma_start(
-                    out=w_planes[32 * quad : 32 * quad + 4, groups, :].bitcast(I32),
-                    in_=W_scales[groups, 4 * quad : 4 * quad + 4, :].rearrange("g r n -> r g n").bitcast(I32),
-                )
+            return x_sb
 
         def load_words(tile_ap, node, count):
             nc.sync.dma_start(
@@ -99,18 +103,23 @@ def tile_softtreeensemble_pa_e_kernel(tc, x, W_words, W_scales, b, leaf_w, out):
             )
             return lw_sb
 
-        load_scale_rows(0, 15)
         w_head = const.tile([P, 7, HALVES, TREES], U32, align_bytes=64)
-        load_words(w_head[:, 0:1, :, :], 0, 1)
-        load_words(w_head[:, 1:3, :, :], 1, 2)
+        x_rows = [load_x(0), load_x(1)]
+        load_words(w_head[:, 0:3, :, :], 0, 3)
+        x_rows.append(load_x(2))
+        load_scale_rows(0, 7)
+        x_rows.append(load_x(3))
         load_words(w_head[:, 3:7, :, :], 3, 4)
+        load_scale_rows(7, 8)
         w_l3 = [load_quad(7), load_quad(11)]
-        load_scale_rows(15, 16)
+        load_scale_rows(15, 24)
+        load_scale_rows(39, 24)
         w_l4 = {0: load_quad(15)}
-        load_scale_rows(31, 32)
 
         x_codes = const.tile([P, HALVES, BATCH], U32, align_bytes=64)
         x_scales = const.tile([P, HALVES, BATCH], U8, align_bytes=64)
+        bias = const.tile([P, P], F32)
+        bias_negated = const.tile([P, P], F32)
         for bt in range(BATCH_TILES):
             x_words = x_rows[bt][:].bitcast(F32)
             xT = bank_pool.tile([P, HALVES, 2, P], F32, tag="bank")
@@ -130,13 +139,11 @@ def tile_softtreeensemble_pa_e_kernel(tc, x, W_words, W_scales, b, leaf_w, out):
                 nc.vector.quantize_mx(
                     out=x_codes[:, h, cols].bitcast(FP8X4), scales=x_scales[:, h, cols], in_=x_grouped[:, h, :]
                 )
-
-        bT = bank_pool.tile([P, P], BF16, tag="bank")
-        nc.tensor.transpose(bT[:], b_rows[:], ident_bf16[:])
-        bias = const.tile([P, P], F32)
-        nc.vector.tensor_copy(out=bias[:], in_=bT[:])
-        bias_negated = const.tile([P, P], F32)
-        nc.vector.tensor_scalar_mul(out=bias_negated[:], in0=bT[:], scalar1=-1.0)
+            if bt == 1:
+                bT = bank_pool.tile([P, P], BF16, tag="bank")
+                nc.tensor.transpose(bT[:], b_rows[:], ident_bf16[:])
+                nc.vector.tensor_copy(out=bias[:], in_=bT[:])
+                nc.vector.tensor_scalar_mul(out=bias_negated[:], in0=bT[:], scalar1=-1.0)
 
         whole = slice(0, BATCH)
 

from contextlib import ExitStack

import concourse.mybir as mybir
from concourse.masks import make_identity

F32 = mybir.dt.float32
BF16 = mybir.dt.bfloat16
I32 = mybir.dt.int32
U32 = mybir.dt.uint32
U8 = mybir.dt.uint8
FP8X4 = mybir.dt.float8_e4m3fn_x4
SIGMOID = mybir.ActivationFunctionType.Sigmoid
MULT = mybir.AluOpType.mult

P = 128
PACK = 4
K_PASS = P * PACK

BATCH, FEATURES, TREES, DEPTH, OUT_COLS = 512, 1024, 128, 6, 128
NODES = 2**DEPTH - 1
LEAVES = 2**DEPTH
HALVES = FEATURES // K_PASS
BATCH_TILES = BATCH // P
LEAF_PASSES = LEAVES // PACK
RUN = 4
QUAD = 4
BLOCKS = 4
PIN_VECTOR = True
WARM_MATMULS = 4
HALF = BATCH // 2

FLOPS = 2 * BATCH * FEATURES * NODES * TREES + 2 * BATCH * LEAVES * TREES * OUT_COLS


def tile_softtreeensemble_pa_e_kernel(tc, x, W_words, W_scales, b, leaf_w, out):
    nc = tc.nc
    with ExitStack() as ctx:
        const = ctx.enter_context(tc.tile_pool(name="const", bufs=1))
        x_pool = ctx.enter_context(tc.tile_pool(name="x_pool", bufs=BATCH_TILES))
        w_pool = ctx.enter_context(tc.tile_pool(name="w_pool", bufs=4))
        lw_pool = ctx.enter_context(tc.tile_pool(name="lw_pool", bufs=2))
        gate_pool = ctx.enter_context(tc.tile_pool(name="gate_pool", bufs=6))
        kids_pool = ctx.enter_context(tc.tile_pool(name="kids_pool", bufs=3))
        leaf_pool = ctx.enter_context(tc.tile_pool(name="leaf_pool", bufs=2))
        acc_pool = ctx.enter_context(tc.psum_pool(name="acc_pool", bufs=1))
        bank_pool = ctx.enter_context(tc.psum_pool(name="bank_pool", bufs=4))
        if PIN_VECTOR:
            ctx.enter_context(tc.manual_schedule(engines={mybir.EngineType.DVE, mybir.EngineType.SP}))

        w_planes = const.tile([P, HALVES * NODES, TREES], U8, align_bytes=64)

        def zero_scale_planes(node, count):
            nc.vector.memset(w_planes[:, HALVES * node : HALVES * (node + count), :].bitcast(I32), 0)

        def load_scale_rows(node, count):
            groups = slice(HALVES * node, HALVES * (node + count))
            for quad in range(4):
                nc.sync.dma_start(
                    out=w_planes[32 * quad : 32 * quad + 4, groups, :].bitcast(I32),
                    in_=W_scales[groups, 4 * quad : 4 * quad + 4, :].rearrange("g r n -> r g n").bitcast(I32),
                )

        zero_scale_planes(0, 7)
        zeros = const.tile([P, BATCH], BF16)
        nc.vector.memset(zeros[:], 0.0)
        idle_bank = bank_pool.tile([P, BATCH], F32, tag="bank")
        for k in range(WARM_MATMULS):
            nc.tensor.matmul(out=idle_bank[:], lhsT=zeros[:, :P], rhs=zeros[:], start=True, stop=True)
        warm = const.tile([P, 1], F32)
        nc.vector.memset(warm[:], 0.0)
        nc.scalar.activation(out=warm[:], in_=warm[:], func=SIGMOID)
        zero_scale_planes(7, 8)
        zero_scale_planes(15, 48)

        ident_f32 = const.tile([P, P], F32)
        make_identity(nc, ident_f32[:])
        b_rows = const.tile([P, P], BF16)
        nc.gpsimd.memset(b_rows[:], 0.0)
        nc.gpsimd.dma_start(out=b_rows[:NODES, :], in_=b)
        ident_bf16 = const.tile([P, P], BF16)
        make_identity(nc, ident_bf16[:])

        def load_x(bt):
            x_sb = x_pool.tile([P, FEATURES], BF16, name="x_sb")
            nc.sync.dma_start(out=x_sb[:], in_=x[bt * P : (bt + 1) * P, :])
            return x_sb

        def load_words(tile_ap, node, count):
            nc.sync.dma_start(
                out=tile_ap.rearrange("p m h n -> p (m h) n").bitcast(I32),
                in_=W_words[HALVES * node : HALVES * (node + count)].rearrange("g p n t -> p g (n t)").bitcast(I32),
            )

        def load_quad(node):
            w_words = w_pool.tile([P, QUAD, HALVES, TREES], U32, name="w_words", align_bytes=64)
            load_words(w_words[:], node, QUAD)
            return w_words

        def load_leaf_weights(group):
            lw_sb = lw_pool.tile([P, 2 * QUAD, TREES], BF16, name="lw_sb", bufs=3)
            nc.sync.dma_start(
                out=lw_sb[:], in_=leaf_w[8 * group : 8 * group + 8].rearrange("j c t -> c j t")
            )
            return lw_sb

        w_head = const.tile([P, 7, HALVES, TREES], U32, align_bytes=64)
        x_rows = [load_x(0), load_x(1)]
        load_words(w_head[:, 0:3, :, :], 0, 3)
        x_rows.append(load_x(2))
        load_scale_rows(0, 7)
        x_rows.append(load_x(3))
        load_words(w_head[:, 3:7, :, :], 3, 4)
        load_scale_rows(7, 8)
        w_l3 = [load_quad(7), load_quad(11)]
        load_scale_rows(15, 24)
        load_scale_rows(39, 24)
        w_l4 = {0: load_quad(15)}

        x_codes = const.tile([P, HALVES, BATCH], U32, align_bytes=64)
        x_scales = const.tile([P, HALVES, BATCH], U8, align_bytes=64)
        bias = const.tile([P, P], F32)
        bias_negated = const.tile([P, P], F32)
        for bt in range(BATCH_TILES):
            x_words = x_rows[bt][:].bitcast(F32)
            xT = bank_pool.tile([P, HALVES, 2, P], F32, tag="bank")
            for h in range(HALVES):
                for u in range(2):
                    nc.tensor.transpose(
                        xT[:, h, u, :], x_words[:, 256 * h + u : 256 * (h + 1) : 2], ident_f32[:]
                    )
            x_grouped = x_pool.tile([P, HALVES, P * PACK], BF16, name="x_grouped", align_bytes=64, bufs=2)
            grouped_words = x_grouped[:].bitcast(F32).rearrange("p h (i u) -> p h i u", u=2)
            if bt % 2 == 0:
                nc.vector.tensor_copy(out=grouped_words, in_=xT[:].rearrange("p h u i -> p h i u"))
            else:
                nc.scalar.copy(out=grouped_words, in_=xT[:].rearrange("p h u i -> p h i u"))
            cols = slice(bt * P, (bt + 1) * P)
            for h in range(HALVES):
                nc.vector.quantize_mx(
                    out=x_codes[:, h, cols].bitcast(FP8X4), scales=x_scales[:, h, cols], in_=x_grouped[:, h, :]
                )
            if bt == 1:
                bT = bank_pool.tile([P, P], BF16, tag="bank")
                nc.tensor.transpose(bT[:], b_rows[:], ident_bf16[:])
                nc.vector.tensor_copy(out=bias[:], in_=bT[:])
                nc.vector.tensor_scalar_mul(out=bias_negated[:], in0=bT[:], scalar1=-1.0)

        whole = slice(0, BATCH)

        def node_z(node, words, slot, cols=whole):
            z = bank_pool.tile([P, cols.stop - cols.start], F32, tag="bank")
            for h in range(HALVES):
                nc.tensor.matmul_mx(
                    out=z[:],
                    lhsT=words[:, slot, h, :].bitcast(FP8X4),
                    lhsT_scale=w_planes[:, HALVES * node + h, :],
                    rhs=x_codes[:, h, cols].bitcast(FP8X4),
                    rhs_scale=x_scales[:, h, cols],
                    start=(h == 0),
                    stop=(h == HALVES - 1),
                )
            return z

        def left_gate(dst, z, node):
            nc.scalar.activation(out=dst, in_=z[:], func=SIGMOID, bias=bias[:, node : node + 1], scale=1.0)

        def right_gate(dst, z, node):
            nc.scalar.activation(
                out=dst, in_=z[:], func=SIGMOID, bias=bias_negated[:, node : node + 1], scale=-1.0
            )

        def gate_tile():
            return gate_pool.tile([P, QUAD, BATCH], F32, name="gate")

        def left_gates(node, count, words, first_slot):
            gate = gate_tile()
            for j in range(count):
                left_gate(gate[:, j, :], node_z(node + j, words, first_slot + j), node + j)
            return gate

        def both_gates(node, words):
            left_tile = gate_tile()
            right_tile = gate_tile()
            for j in range(QUAD):
                z = node_z(node + j, words, j)
                left_gate(left_tile[:, j, :], z, node + j)
                right_gate(right_tile[:, j, :], z, node + j)
            return left_tile, right_tile

        def transpose_leaf_weights(lw_sb, lw_grouped, half):
            lwT = bank_pool.tile([P, 2 * QUAD, OUT_COLS], BF16, tag="bank")
            for j in range(2 * QUAD):
                nc.tensor.transpose(lwT[:, j, :], lw_sb[:, j, :], ident_bf16[:])
            nc.scalar.copy(
                out=lw_grouped[:, 2 * half : 2 * half + 2, :].rearrange("p q (c t) -> p q c t", t=PACK),
                in_=lwT[:].rearrange("p (t q) c -> p q c t", t=PACK),
            )

        def group_leaf_weights(raw):
            lw_grouped = lw_pool.tile([P, 4, OUT_COLS * PACK], BF16, name="lw_grouped", align_bytes=64)
            for half in range(2):
                transpose_leaf_weights(raw[half], lw_grouped, half)
            return lw_grouped

        def quantise_leaf_weights(lw_grouped):
            lw_codes = lw_pool.tile([P, 4 * OUT_COLS], U32, name="lw_codes", align_bytes=64)
            lw_scales = lw_pool.tile([P, 4 * OUT_COLS], U8, name="lw_scales", align_bytes=64)
            nc.vector.quantize_mx(
                out=lw_codes[:].bitcast(FP8X4), scales=lw_scales[:], in_=lw_grouped[:].rearrange("p q n -> p (q n)")
            )
            return lw_codes, lw_scales

        def kids_tile(count):
            return kids_pool.tile([P, count, 2, BATCH], F32, name="kids")

        def as_row(kids):
            return kids[:].rearrange("p j s i -> p (j s) i")

        def lefts(parents, gate, kids, nodes, cols=whole):
            nc.vector.tensor_mul(out=kids[:, nodes, 0, cols], in0=parents, in1=gate[:, nodes, cols])

        def rights(parents, kids, nodes, cols=whole):
            nc.vector.tensor_sub(out=kids[:, nodes, 1, cols], in0=parents, in1=kids[:, nodes, 0, cols])

        def leaf_products(p6_pair, side, parents, gate):
            nc.vector.tensor_tensor(
                out=p6_pair[:, side, :].rearrange("p (c i a) -> p c a i", i=RUN, a=PACK),
                in0=parents.rearrange("p a (c i) -> p c a i", i=RUN),
                in1=gate[:].rearrange("p a (c i) -> p c a i", i=RUN),
                op=MULT,
            )

        acc = [acc_pool.tile([P, BATCH], F32, name="acc%d" % bt) for bt in range(BATCH_TILES)]

        def quantise_and_contract(first_pass, p6_pair, lw):
            p6_codes = leaf_pool.tile([P, 2 * BATCH], U32, name="p6_codes", align_bytes=64)
            p6_scales = leaf_pool.tile([P, 2 * BATCH], U8, name="p6_scales", align_bytes=64)
            nc.vector.quantize_mx(
                out=p6_codes[:].bitcast(FP8X4), scales=p6_scales[:], in_=p6_pair[:].rearrange("p s n -> p (s n)")
            )
            for side in range(2):
                leaf_pass = first_pass + side
                out_cols = slice((leaf_pass % 4) * OUT_COLS, (leaf_pass % 4 + 1) * OUT_COLS)
                for bt in range(BATCH_TILES):
                    rows = slice(side * BATCH + bt * P, side * BATCH + (bt + 1) * P)
                    nc.tensor.matmul_mx(
                        out=acc[bt][:, :OUT_COLS],
                        lhsT=p6_codes[:, rows].bitcast(FP8X4),
                        lhsT_scale=p6_scales[:, rows],
                        rhs=lw[0][:, out_cols].bitcast(FP8X4),
                        rhs_scale=lw[1][:, out_cols],
                        start=(leaf_pass == 0),
                        stop=(leaf_pass == LEAF_PASSES - 1),
                    )

        p1 = gate_pool.tile([P, 2, BATCH], F32, name="gate")
        g1 = gate_pool.tile([P, 2, BATCH], F32, name="gate")
        g2 = gate_tile()
        kids2 = kids_tile(2)
        kids3 = kids_tile(4)
        halves = [slice(0, HALF), slice(HALF, BATCH)]

        def first_gates(cols):
            z0 = node_z(0, w_head, 0, cols)
            left_gate(p1[:, 0, cols], z0, 0)
            left_gate(g1[:, 0, cols], node_z(1, w_head, 1, cols), 1)
            right_gate(p1[:, 1, cols], z0, 0)
            left_gate(g1[:, 1, cols], node_z(2, w_head, 2, cols), 2)

        def level2_gates(cols):
            for j in range(4):
                left_gate(g2[:, j, cols], node_z(3 + j, w_head, 3 + j, cols), 3 + j)

        def level1_products(cols):
            for j in range(2):
                lefts(p1[:, j : j + 1, cols], g1, kids2, slice(j, j + 1), cols)
            for j in range(2):
                rights(p1[:, j : j + 1, cols], kids2, slice(j, j + 1), cols)

        def level2_products(cols):
            for k in range(2):
                lefts(as_row(kids2)[:, 2 * k : 2 * k + 2, cols], g2, kids3, slice(2 * k, 2 * k + 2), cols)
            for k in range(2):
                rights(as_row(kids2)[:, 2 * k : 2 * k + 2, cols], kids3, slice(2 * k, 2 * k + 2), cols)

        first_gates(halves[0])
        first_gates(halves[1])
        level1_products(halves[0])
        level2_gates(halves[0])
        level1_products(halves[1])
        level2_gates(halves[1])
        g3 = [left_gates(7 + 4 * k, 4, w_l3[k], 0) for k in range(2)]
        w_l5 = {0: load_quad(31), 1: load_quad(35)}
        lw_raw = {0: [load_leaf_weights(0), load_leaf_weights(1)]}
        level2_products(halves[0])
        level2_products(halves[1])

        g4 = {0: left_gates(15, 4, w_l4[0], 0)}
        w_l4[1] = load_quad(19)

        kids4 = [const.tile([P, QUAD, 2, BATCH], F32, name="kids4_%d" % k) for k in range(2)]
        for k in range(2):
            lefts(as_row(kids3)[:, 4 * k : 4 * k + 4, :], g3[k], kids4[k], slice(0, 4))
        for k in range(2):
            rights(as_row(kids3)[:, 4 * k : 4 * k + 4, :], kids4[k], slice(0, 4))

        def level4_parents(block):
            return as_row(kids4[block // 2])[:, 4 * (block % 2) : 4 * (block % 2) + 4, :]

        g5 = {}
        kids5 = {}

        def make_level5_gates(block, half):
            g5[(block, half)] = both_gates(31 + 8 * block + 4 * half, w_l5[2 * block + half])

        make_level5_gates(0, 0)
        kids5[0] = kids_tile(4)
        for k in range(2):
            lefts(level4_parents(0)[:, 2 * k : 2 * k + 2, :], g4[0], kids5[0], slice(2 * k, 2 * k + 2))
        for k in range(2):
            rights(level4_parents(0)[:, 2 * k : 2 * k + 2, :], kids5[0], slice(2 * k, 2 * k + 2))

        def pair_products(block, half):
            p6_pair = leaf_pool.tile([P, 2, BATCH * PACK], BF16, name="p6_pair", align_bytes=64)
            for side in range(2):
                leaf_products(
                    p6_pair, side, as_row(kids5[block])[:, 4 * half : 4 * half + 4, :], g5[(block, half)][side]
                )
            return p6_pair

        for block in range(BLOCKS):
            following = block + 1
            make_level5_gates(block, 1)
            if following < BLOCKS:
                w_l5[2 * following] = load_quad(31 + 8 * following)
                w_l5[2 * following + 1] = load_quad(35 + 8 * following)
                lw_raw[following] = [load_leaf_weights(2 * following), load_leaf_weights(2 * following + 1)]
                g4[following] = left_gates(15 + 4 * following, 4, w_l4[following], 0)
                if following + 1 < BLOCKS:
                    w_l4[following + 1] = load_quad(15 + 4 * (following + 1))
            first_pair = pair_products(block, 0)
            lw_grouped = group_leaf_weights(lw_raw[block])
            if following < BLOCKS:
                kids5[following] = kids_tile(4)
                lefts(level4_parents(following), g4[following], kids5[following], slice(0, 4))
                make_level5_gates(following, 0)
            second_pair = pair_products(block, 1)
            if following < BLOCKS:
                rights(level4_parents(following), kids5[following], slice(0, 4))
            lw = quantise_leaf_weights(lw_grouped)
            quantise_and_contract(4 * block, first_pair, lw)
            quantise_and_contract(4 * block + 2, second_pair, lw)

        out_sb = const.tile([P, BATCH_TILES, OUT_COLS], F32)
        for bt in range(BATCH_TILES):
            if bt % 2 == 0:
                nc.vector.tensor_copy(out=out_sb[:, bt, :], in_=acc[bt][:, :OUT_COLS])
            else:
                nc.scalar.copy(out=out_sb[:, bt, :], in_=acc[bt][:, :OUT_COLS])
        nc.sync.dma_start(out=out.rearrange("(bt p) c -> p bt c", p=P), in_=out_sb[:])
